import numpy as np
import ml_dtypes


def mxq(x, axis, fmt="e4m3"):
    dtype, down = {"e4m3": (ml_dtypes.float8_e4m3fn, 7), "e5m2": (ml_dtypes.float8_e5m2, 14)}[fmt]
    v = np.moveaxis(np.asarray(x, np.float32).astype(ml_dtypes.bfloat16).astype(np.float64), axis, -1)
    blocks = v.reshape(v.shape[:-1] + (-1, 32))
    amax = np.abs(blocks).max(-1, keepdims=True)
    byte = np.maximum(np.where(amax > 0, np.frexp(amax)[1] - 1 + 127, 0) - down, 1)
    scale = np.exp2(byte - 127.0)
    codes = (blocks / scale).astype(np.float32).astype(dtype).astype(np.float64)
    return np.moveaxis((codes * scale).reshape(v.shape), -1, axis)


WIDE = False


def mx_kscale(k):
    if not WIDE:
        return np.ones(k)
    levels = np.array([20, -20, 10, -10, 0])
    a = np.random.permutation(np.resize(levels, k // 512 * 4)).reshape(k // 512, 4)
    idx = np.arange(k)
    return np.exp2(a[idx // 512, idx % 128 // 32])


BF16 = ml_dtypes.bfloat16


def bf(x):
    return np.asarray(x, np.float32).astype(BF16)


def f64(x):
    return np.asarray(x).astype(np.float64)


T, K, E, H, KVH, D = 512, 1024, 2048, 16, 4, 128
EPS = 1e-05


def setup_inputs():
    s = mx_kscale(T)
    x0 = bf(np.random.standard_normal((T, E)))
    Wq = bf(np.random.standard_normal((H * D, E)) / np.sqrt(E))
    q_norm_w = bf(1.5 + 0.1 * np.random.standard_normal(D))
    g = bf(np.random.standard_normal((H, T, D)) * np.exp2(np.random.randint(-12, 1, (1, T, 1))) / s[None, :, None])
    q = f64(x0) @ f64(Wq).T
    rstd = 1.0 / np.sqrt(np.mean(np.square(q.reshape(T, H, D)), axis=-1) + EPS)
    return {"hidden_states": bf(f64(x0) * s[:, None]), "Wq": Wq, "q_norm_w": q_norm_w,
            "q": np.asarray(q, np.float32), "rstd": np.asarray(rstd, np.float32), "grad_out": g}


def reference(hidden_states, Wq, q_norm_w, q, rstd, grad_out):
    qh = f64(q).reshape(T, H, D)
    r = f64(rstd)[:, :, None]
    gw = f64(grad_out).transpose(1, 0, 2) * f64(q_norm_w)
    m = np.mean(gw * qh, axis=-1, keepdims=True)
    dq = (r * gw - qh * (r * r * r) * m).reshape(T, H * D)
    return mxq(dq, 0, "e5m2").T @ mxq(f64(hidden_states), 0, "e4m3")

@@ -1,0 +1,176 @@
+from contextlib import ExitStack
+
+import concourse.mybir as mybir
+
+F32 = mybir.dt.float32
+BF16 = mybir.dt.bfloat16
+U32 = mybir.dt.uint32
+U8 = mybir.dt.uint8
+E4M3_X4 = mybir.dt.float8_e4m3fn_x4
+E5M2_X4 = mybir.dt.float8_e5m2_x4
+MULT = mybir.AluOpType.mult
+ADD = mybir.AluOpType.add
+
+P = 128
+PACK = 4
+T = P * PACK
+H = 16
+D = 128
+E = 2048
+N_TILE = 512
+N_TILES = E // N_TILE
+RUN = 4
+HEADS_PER_LOAD = 4
+HIDDEN_LOADS = 2
+
+FLOPS = 2 * T * H * D * E
+BYTES = 2 * T * E + 2 * D + 4 * T * H * D + 4 * T * H + 2 * H * T * D + 4 * H * D * E
+
+
+def regrouped(by_column):
+    return by_column.rearrange("p (c i) j -> p c j i", i=RUN)
+
+
+def in_runs(by_token):
+    return by_token.rearrange("p j (c i) -> p c j i", i=RUN)
+
+
+def tile_combcrossattention_pa_v_kernel(
+    tc, hidden_states, Wq, q_norm_w, q, rstd, grad_out, out
+):
+    nc = tc.nc
+    with ExitStack() as ctx:
+        keep = ctx.enter_context(tc.tile_pool(name="keep", bufs=1))
+        work = ctx.enter_context(tc.tile_pool(name="work", bufs=3))
+        rows = ctx.enter_context(tc.tile_pool(name="rows", bufs=4))
+        banks = ctx.enter_context(tc.psum_pool(name="banks", bufs=8))
+
+        gain = keep.tile([P, D], BF16)
+        rstd_sb = keep.tile([P, PACK, H], F32)
+        grad_sb = keep.tile([P, H, PACK, D], BF16)
+        q_sb = keep.tile([P, PACK, H * D], F32)
+        hidden_sb = keep.tile([P, PACK, E], BF16)
+
+        grad_view = grad_out.rearrange("h (p j) d -> p h j d", j=PACK)
+        q_view = q.rearrange("(p j) c -> p j c", j=PACK)
+        hidden_view = hidden_states.rearrange("(p j) e -> p j e", j=PACK)
+
+        def load_heads(first):
+            heads = slice(first, first + HEADS_PER_LOAD)
+            cols = slice(first * D, (first + HEADS_PER_LOAD) * D)
+            nc.sync.dma_start(out=grad_sb[:, heads, :, :], in_=grad_view[:, heads, :, :])
+            nc.sync.dma_start(out=q_sb[:, :, cols], in_=q_view[:, :, cols])
+
+        nc.scalar.dma_start(out=gain[:], in_=q_norm_w.partition_broadcast(P))
+        nc.sync.dma_start(out=rstd_sb[:], in_=rstd.rearrange("(p j) h -> p j h", j=PACK))
+        load_heads(0)
+        for part in range(HIDDEN_LOADS):
+            cols = slice(part * (E // HIDDEN_LOADS), (part + 1) * (E // HIDDEN_LOADS))
+            nc.sync.dma_start(out=hidden_sb[:, :, cols], in_=hidden_view[:, :, cols])
+        for first in range(HEADS_PER_LOAD, H, HEADS_PER_LOAD):
+            load_heads(first)
+
+        hidden_grouped = keep.tile([P, E, PACK], BF16, align_bytes=64)
+        hidden_codes = keep.tile([P, E], U32, align_bytes=64)
+        hidden_scales = keep.tile([P, E], U8, align_bytes=64)
+
+        def regroup_hidden(n):
+            cols = slice(n * N_TILE, (n + 1) * N_TILE)
+            nc.scalar.copy(
+                out=regrouped(hidden_grouped[:, cols, :]), in_=in_runs(hidden_sb[:, :, cols])
+            )
+
+        def quantise_hidden(n):
+            cols = slice(n * N_TILE, (n + 1) * N_TILE)
+            nc.vector.quantize_mx(
+                out=hidden_codes[:, cols].bitcast(E4M3_X4),
+                scales=hidden_scales[:, cols],
+                in_=hidden_grouped[:, cols, :].rearrange("p w j -> p (w j)"),
+            )
+
+        minus_r2_over_d = keep.tile([P, PACK, H], F32)
+        nc.vector.scalar_tensor_tensor(
+            out=minus_r2_over_d[:], in0=rstd_sb[:], scalar=-1.0 / D, in1=rstd_sb[:],
+            op0=MULT, op1=MULT,
+        )
+        dq_codes = keep.tile([P, H * D], U32, align_bytes=64)
+        dq_scales = keep.tile([P, H * D], U8, align_bytes=64)
+
+        def scaled_gradient(h):
+            v = work.tile([P, PACK, D], F32)
+            for j in range(PACK):
+                nc.vector.scalar_tensor_tensor(
+                    out=v[:, j, :], in0=grad_sb[:, h, j, :], scalar=rstd_sb[:, j, h : h + 1],
+                    in1=gain[:], op0=MULT, op1=MULT,
+                )
+            return v
+
+        def coefficient(h, v):
+            coef = work.tile([P, PACK], F32)
+            products = work.tile([P, PACK, D], F32)
+            for j in range(PACK):
+                nc.vector.scalar_tensor_tensor(
+                    out=products[:, j, :], in0=v[:, j, :],
+                    scalar=minus_r2_over_d[:, j, h : h + 1],
+                    in1=q_sb[:, j, h * D : (h + 1) * D], op0=MULT, op1=MULT,
+                    accum_out=coef[:, j : j + 1],
+                )
+            return coef
+
+        def head_gradient(h, v, coef):
+            dq = work.tile([P, PACK, D], BF16)
+            for j in range(PACK):
+                nc.vector.scalar_tensor_tensor(
+                    out=dq[:, j, :], in0=q_sb[:, j, h * D : (h + 1) * D],
+                    scalar=coef[:, j : j + 1], in1=v[:, j, :], op0=MULT, op1=ADD,
+                )
+            return dq
+
+        def regroup_head(dq):
+            dq_grouped = work.tile([P, D, PACK], BF16, align_bytes=64)
+            nc.vector.tensor_copy(out=regrouped(dq_grouped[:]), in_=in_runs(dq[:]))
+            return dq_grouped
+
+        def quantise_head(h, dq_grouped):
+            cols = slice(h * D, (h + 1) * D)
+            nc.vector.quantize_mx(
+                out=dq_codes[:, cols].bitcast(E5M2_X4),
+                scales=dq_scales[:, cols],
+                in_=dq_grouped[:].rearrange("p d j -> p (d j)"),
+            )
+
+        def multiply_head(h):
+            head_cols = slice(h * D, (h + 1) * D)
+            out_rows = rows.tile([P, E], F32)
+            for n in range(N_TILES):
+                cols = slice(n * N_TILE, (n + 1) * N_TILE)
+                acc = banks.tile([P, N_TILE], F32)
+                nc.tensor.matmul_mx(
+                    out=acc[:],
+                    lhsT=dq_codes[:, head_cols].bitcast(E5M2_X4),
+                    lhsT_scale=dq_scales[:, head_cols],
+                    rhs=hidden_codes[:, cols].bitcast(E4M3_X4),
+                    rhs_scale=hidden_scales[:, cols],
+                    start=True,
+                    stop=True,
+                )
+                nc.scalar.copy(out=out_rows[:, cols], in_=acc[:])
+            nc.sync.dma_start(out=out[head_cols, :], in_=out_rows[:])
+
+        for n in range(N_TILES):
+            regroup_hidden(n)
+            quantise_hidden(n)
+
+        dq = None
+        for h in range(H + 1):
+            if h < H:
+                v = scaled_gradient(h)
+            if h > 0:
+                dq_grouped = regroup_head(dq)
+            if h < H:
+                coef = coefficient(h, v)
+            if h > 0:
+                quantise_head(h - 1, dq_grouped)
+                multiply_head(h - 1)
+            if h < H:
+                dq = head_gradient(h, v, coef)

@@ -22,6 +22,7 @@ N_TILES = E // N_TILE
 RUN = 4
 HEADS_PER_LOAD = 4
 HIDDEN_LOADS = 2
+HIDDEN_LAG = 2
 
 FLOPS = 2 * T * H * D * E
 BYTES = 2 * T * E + 2 * D + 4 * T * H * D + 4 * T * H + 2 * H * T * D + 4 * H * D * E
@@ -157,20 +158,24 @@ def tile_combcrossattention_pa_v_kernel(
                 nc.scalar.copy(out=out_rows[:, cols], in_=acc[:])
             nc.sync.dma_start(out=out[head_cols, :], in_=out_rows[:])
 
-        for n in range(N_TILES):
-            regroup_hidden(n)
-            quantise_hidden(n)
+        with tc.manual_schedule():
+            for n in range(N_TILES):
+                regroup_hidden(n)
 
-        dq = None
-        for h in range(H + 1):
-            if h < H:
-                v = scaled_gradient(h)
-            if h > 0:
-                dq_grouped = regroup_head(dq)
-            if h < H:
-                coef = coefficient(h, v)
-            if h > 0:
-                quantise_head(h - 1, dq_grouped)
-                multiply_head(h - 1)
-            if h < H:
-                dq = head_gradient(h, v, coef)
+            dq = None
+            for h in range(H + 1):
+                if h < H:
+                    v = scaled_gradient(h)
+                if h > 0:
+                    dq_grouped = regroup_head(dq)
+                if h < H:
+                    coef = coefficient(h, v)
+                if h > 0:
+                    quantise_head(h - 1, dq_grouped)
+                if 0 <= h - HIDDEN_LAG < N_TILES:
+                    quantise_hidden(h - HIDDEN_LAG)
+                if h < H:
+                    dq = head_gradient(h, v, coef)
+
+            for h in range(H):
+                multiply_head(h)

@@ -22,7 +22,6 @@ N_TILES = E // N_TILE
 RUN = 4
 HEADS_PER_LOAD = 4
 HIDDEN_LOADS = 2
-HIDDEN_LAG = 2
 
 FLOPS = 2 * T * H * D * E
 BYTES = 2 * T * E + 2 * D + 4 * T * H * D + 4 * T * H + 2 * H * T * D + 4 * H * D * E
@@ -64,11 +63,10 @@ def tile_combcrossattention_pa_v_kernel(
 
         nc.scalar.dma_start(out=gain[:], in_=q_norm_w.partition_broadcast(P))
         nc.sync.dma_start(out=rstd_sb[:], in_=rstd.rearrange("(p j) h -> p j h", j=PACK))
-        load_heads(0)
         for part in range(HIDDEN_LOADS):
             cols = slice(part * (E // HIDDEN_LOADS), (part + 1) * (E // HIDDEN_LOADS))
             nc.sync.dma_start(out=hidden_sb[:, :, cols], in_=hidden_view[:, :, cols])
-        for first in range(HEADS_PER_LOAD, H, HEADS_PER_LOAD):
+        for first in range(0, H, HEADS_PER_LOAD):
             load_heads(first)
 
         hidden_grouped = keep.tile([P, E, PACK], BF16, align_bytes=64)
@@ -77,9 +75,8 @@ def tile_combcrossattention_pa_v_kernel(
 
         def regroup_hidden(n):
             cols = slice(n * N_TILE, (n + 1) * N_TILE)
-            nc.scalar.copy(
-                out=regrouped(hidden_grouped[:, cols, :]), in_=in_runs(hidden_sb[:, :, cols])
-            )
+            copy = nc.vector.tensor_copy if n % 2 == 0 else nc.scalar.copy
+            copy(out=regrouped(hidden_grouped[:, cols, :]), in_=in_runs(hidden_sb[:, :, cols]))
 
         def quantise_hidden(n):
             cols = slice(n * N_TILE, (n + 1) * N_TILE)
@@ -158,24 +155,21 @@ def tile_combcrossattention_pa_v_kernel(
                 nc.scalar.copy(out=out_rows[:, cols], in_=acc[:])
             nc.sync.dma_start(out=out[head_cols, :], in_=out_rows[:])
 
-        with tc.manual_schedule():
-            for n in range(N_TILES):
-                regroup_hidden(n)
+        for n in range(N_TILES):
+            regroup_hidden(n)
+        for n in range(N_TILES):
+            quantise_hidden(n)
 
-            dq = None
-            for h in range(H + 1):
-                if h < H:
-                    v = scaled_gradient(h)
-                if h > 0:
-                    dq_grouped = regroup_head(dq)
-                if h < H:
-                    coef = coefficient(h, v)
-                if h > 0:
-                    quantise_head(h - 1, dq_grouped)
-                if 0 <= h - HIDDEN_LAG < N_TILES:
-                    quantise_hidden(h - HIDDEN_LAG)
-                if h < H:
-                    dq = head_gradient(h, v, coef)
-
-            for h in range(H):
-                multiply_head(h)
+        dq = None
+        for h in range(H + 1):
+            if h < H:
+                v = scaled_gradient(h)
+            if h > 0:
+                dq_grouped = regroup_head(dq)
+            if h < H:
+                coef = coefficient(h, v)
+            if h > 0:
+                quantise_head(h - 1, dq_grouped)
+                multiply_head(h - 1)
+            if h < H:
+                dq = head_gradient(h, v, coef)

@@ -20,7 +20,6 @@ E = 2048
 N_TILE = 512
 N_TILES = E // N_TILE
 RUN = 4
-HEADS_PER_LOAD = 4
 HIDDEN_LOADS = 2
 
 FLOPS = 2 * T * H * D * E
@@ -55,9 +54,9 @@ def tile_combcrossattention_pa_v_kernel(
         q_view = q.rearrange("(p j) c -> p j c", j=PACK)
         hidden_view = hidden_states.rearrange("(p j) e -> p j e", j=PACK)
 
-        def load_heads(first):
-            heads = slice(first, first + HEADS_PER_LOAD)
-            cols = slice(first * D, (first + HEADS_PER_LOAD) * D)
+        def load_heads(first, count):
+            heads = slice(first, first + count)
+            cols = slice(first * D, (first + count) * D)
             nc.sync.dma_start(out=grad_sb[:, heads, :, :], in_=grad_view[:, heads, :, :])
             nc.sync.dma_start(out=q_sb[:, :, cols], in_=q_view[:, :, cols])
 
@@ -66,8 +65,10 @@ def tile_combcrossattention_pa_v_kernel(
         for part in range(HIDDEN_LOADS):
             cols = slice(part * (E // HIDDEN_LOADS), (part + 1) * (E // HIDDEN_LOADS))
             nc.sync.dma_start(out=hidden_sb[:, :, cols], in_=hidden_view[:, :, cols])
-        for first in range(0, H, HEADS_PER_LOAD):
-            load_heads(first)
+        first, count = 0, 1
+        while first < H:
+            load_heads(first, count)
+            first, count = first + count, first + count
 
         hidden_grouped = keep.tile([P, E, PACK], BF16, align_bytes=64)
         hidden_codes = keep.tile([P, E], U32, align_bytes=64)

@@ -153,7 +153,10 @@ def tile_combcrossattention_pa_v_kernel(
                     start=True,
                     stop=True,
                 )
-                nc.scalar.copy(out=out_rows[:, cols], in_=acc[:])
+                if n < N_TILES - 1:
+                    nc.scalar.copy(out=out_rows[:, cols], in_=acc[:])
+                else:
+                    nc.vector.tensor_copy(out=out_rows[:, cols], in_=acc[:])
             nc.sync.dma_start(out=out[head_cols, :], in_=out_rows[:])
 
         for n in range(N_TILES):

@@ -21,6 +21,7 @@ N_TILE = 512
 N_TILES = E // N_TILE
 RUN = 4
 HIDDEN_LOADS = 2
+HIDDEN_LAG = 1
 
 FLOPS = 2 * T * H * D * E
 BYTES = 2 * T * E + 2 * D + 4 * T * H * D + 4 * T * H + 2 * H * T * D + 4 * H * D * E
@@ -41,10 +42,11 @@ def tile_combcrossattention_pa_v_kernel(
     with ExitStack() as ctx:
         keep = ctx.enter_context(tc.tile_pool(name="keep", bufs=1))
         work = ctx.enter_context(tc.tile_pool(name="work", bufs=3))
-        rows = ctx.enter_context(tc.tile_pool(name="rows", bufs=4))
+        rows = ctx.enter_context(tc.tile_pool(name="rows", bufs=6))
         banks = ctx.enter_context(tc.psum_pool(name="banks", bufs=8))
+        ctx.enter_context(tc.manual_schedule())
 
-        gain = keep.tile([P, D], BF16)
+        gain_row = keep.tile([P, D], BF16)
         rstd_sb = keep.tile([P, PACK, H], F32)
         grad_sb = keep.tile([P, H, PACK, D], BF16)
         q_sb = keep.tile([P, PACK, H * D], F32)
@@ -60,15 +62,23 @@ def tile_combcrossattention_pa_v_kernel(
             nc.sync.dma_start(out=grad_sb[:, heads, :, :], in_=grad_view[:, heads, :, :])
             nc.sync.dma_start(out=q_sb[:, :, cols], in_=q_view[:, :, cols])
 
-        nc.scalar.dma_start(out=gain[:], in_=q_norm_w.partition_broadcast(P))
+        nc.vector.memset(gain_row[:], 0.0)
+        nc.sync.dma_start(out=gain_row[0:1, :], in_=q_norm_w.unsqueeze(0))
         nc.sync.dma_start(out=rstd_sb[:], in_=rstd.rearrange("(p j) h -> p j h", j=PACK))
         for part in range(HIDDEN_LOADS):
             cols = slice(part * (E // HIDDEN_LOADS), (part + 1) * (E // HIDDEN_LOADS))
-            nc.sync.dma_start(out=hidden_sb[:, :, cols], in_=hidden_view[:, :, cols])
+            nc.scalar.dma_start(out=hidden_sb[:, :, cols], in_=hidden_view[:, :, cols])
         first, count = 0, 1
         while first < H:
             load_heads(first, count)
             first, count = first + count, first + count
+
+        ones = keep.tile([P, P], BF16)
+        nc.vector.memset(ones[:], 1.0)
+        acc = banks.tile([P, N_TILE], F32)
+        nc.tensor.matmul(out=acc[:, :D], lhsT=ones[:], rhs=gain_row[:], start=True, stop=True)
+        gain = keep.tile([P, D], F32)
+        nc.vector.tensor_copy(out=gain[:], in_=acc[:, :D])
 
         hidden_grouped = keep.tile([P, E, PACK], BF16, align_bytes=64)
         hidden_codes = keep.tile([P, E], U32, align_bytes=64)
@@ -76,8 +86,9 @@ def tile_combcrossattention_pa_v_kernel(
 
         def regroup_hidden(n):
             cols = slice(n * N_TILE, (n + 1) * N_TILE)
-            copy = nc.vector.tensor_copy if n % 2 == 0 else nc.scalar.copy
-            copy(out=regrouped(hidden_grouped[:, cols, :]), in_=in_runs(hidden_sb[:, :, cols]))
+            nc.scalar.copy(
+                out=regrouped(hidden_grouped[:, cols, :]), in_=in_runs(hidden_sb[:, :, cols])
+            )
 
         def quantise_hidden(n):
             cols = slice(n * N_TILE, (n + 1) * N_TILE)
@@ -153,16 +164,11 @@ def tile_combcrossattention_pa_v_kernel(
                     start=True,
                     stop=True,
                 )
-                if n < N_TILES - 1:
-                    nc.scalar.copy(out=out_rows[:, cols], in_=acc[:])
-                else:
-                    nc.vector.tensor_copy(out=out_rows[:, cols], in_=acc[:])
+                nc.scalar.copy(out=out_rows[:, cols], in_=acc[:])
             nc.sync.dma_start(out=out[head_cols, :], in_=out_rows[:])
 
         for n in range(N_TILES):
             regroup_hidden(n)
-        for n in range(N_TILES):
-            quantise_hidden(n)
 
         dq = None
         for h in range(H + 1):
@@ -174,6 +180,10 @@ def tile_combcrossattention_pa_v_kernel(
                 coef = coefficient(h, v)
             if h > 0:
                 quantise_head(h - 1, dq_grouped)
-                multiply_head(h - 1)
+            if 0 <= h - HIDDEN_LAG < N_TILES:
+                quantise_hidden(h - HIDDEN_LAG)
             if h < H:
                 dq = head_gradient(h, v, coef)
+
+        for h in range(H):
+            multiply_head(h)

@@ -19,6 +19,7 @@ D = 128
 E = 2048
 N_TILE = 512
 N_TILES = E // N_TILE
+BANKS_PER_STORE = 2
 RUN = 4
 HIDDEN_LOADS = 2
 HIDDEN_LAG = 1
@@ -42,7 +43,7 @@ def tile_combcrossattention_pa_v_kernel(
     with ExitStack() as ctx:
         keep = ctx.enter_context(tc.tile_pool(name="keep", bufs=1))
         work = ctx.enter_context(tc.tile_pool(name="work", bufs=3))
-        rows = ctx.enter_context(tc.tile_pool(name="rows", bufs=6))
+        rows = ctx.enter_context(tc.tile_pool(name="rows", bufs=12))
         banks = ctx.enter_context(tc.psum_pool(name="banks", bufs=8))
         ctx.enter_context(tc.manual_schedule())
 
@@ -151,21 +152,29 @@ def tile_combcrossattention_pa_v_kernel(
 
         def multiply_head(h):
             head_cols = slice(h * D, (h + 1) * D)
-            out_rows = rows.tile([P, E], F32)
-            for n in range(N_TILES):
-                cols = slice(n * N_TILE, (n + 1) * N_TILE)
-                acc = banks.tile([P, N_TILE], F32)
-                nc.tensor.matmul_mx(
-                    out=acc[:],
-                    lhsT=dq_codes[:, head_cols].bitcast(E5M2_X4),
-                    lhsT_scale=dq_scales[:, head_cols],
-                    rhs=hidden_codes[:, cols].bitcast(E4M3_X4),
-                    rhs_scale=hidden_scales[:, cols],
-                    start=True,
-                    stop=True,
+            for first_bank in range(0, N_TILES, BANKS_PER_STORE):
+                out_rows = rows.tile([P, BANKS_PER_STORE, N_TILE], F32)
+                for b in range(BANKS_PER_STORE):
+                    n = first_bank + b
+                    cols = slice(n * N_TILE, (n + 1) * N_TILE)
+                    acc = banks.tile([P, N_TILE], F32)
+                    nc.tensor.matmul_mx(
+                        out=acc[:],
+                        lhsT=dq_codes[:, head_cols].bitcast(E5M2_X4),
+                        lhsT_scale=dq_scales[:, head_cols],
+                        rhs=hidden_codes[:, cols].bitcast(E4M3_X4),
+                        rhs_scale=hidden_scales[:, cols],
+                        start=True,
+                        stop=True,
+                    )
+                    if h == H - 1 and b % 2 == 1:
+                        nc.vector.tensor_copy(out=out_rows[:, b, :], in_=acc[:])
+                    else:
+                        nc.scalar.copy(out=out_rows[:, b, :], in_=acc[:])
+                nc.sync.dma_start(
+                    out=out[head_cols, first_bank * N_TILE : (first_bank + BANKS_PER_STORE) * N_TILE],
+                    in_=out_rows[:].rearrange("p b n -> p (b n)"),
                 )
-                nc.scalar.copy(out=out_rows[:, cols], in_=acc[:])
-            nc.sync.dma_start(out=out[head_cols, :], in_=out_rows[:])
 
         for n in range(N_TILES):
             regroup_hidden(n)

@@ -19,10 +19,8 @@ D = 128
 E = 2048
 N_TILE = 512
 N_TILES = E // N_TILE
-BANKS_PER_STORE = 2
 RUN = 4
 HIDDEN_LOADS = 2
-HIDDEN_LAG = 1
 
 FLOPS = 2 * T * H * D * E
 BYTES = 2 * T * E + 2 * D + 4 * T * H * D + 4 * T * H + 2 * H * T * D + 4 * H * D * E
@@ -43,9 +41,8 @@ def tile_combcrossattention_pa_v_kernel(
     with ExitStack() as ctx:
         keep = ctx.enter_context(tc.tile_pool(name="keep", bufs=1))
         work = ctx.enter_context(tc.tile_pool(name="work", bufs=3))
-        rows = ctx.enter_context(tc.tile_pool(name="rows", bufs=12))
+        rows = ctx.enter_context(tc.tile_pool(name="rows", bufs=4))
         banks = ctx.enter_context(tc.psum_pool(name="banks", bufs=8))
-        ctx.enter_context(tc.manual_schedule())
 
         gain_row = keep.tile([P, D], BF16)
         rstd_sb = keep.tile([P, PACK, H], F32)
@@ -68,7 +65,7 @@ def tile_combcrossattention_pa_v_kernel(
         nc.sync.dma_start(out=rstd_sb[:], in_=rstd.rearrange("(p j) h -> p j h", j=PACK))
         for part in range(HIDDEN_LOADS):
             cols = slice(part * (E // HIDDEN_LOADS), (part + 1) * (E // HIDDEN_LOADS))
-            nc.scalar.dma_start(out=hidden_sb[:, :, cols], in_=hidden_view[:, :, cols])
+            nc.sync.dma_start(out=hidden_sb[:, :, cols], in_=hidden_view[:, :, cols])
         first, count = 0, 1
         while first < H:
             load_heads(first, count)
@@ -87,9 +84,8 @@ def tile_combcrossattention_pa_v_kernel(
 
         def regroup_hidden(n):
             cols = slice(n * N_TILE, (n + 1) * N_TILE)
-            nc.scalar.copy(
-                out=regrouped(hidden_grouped[:, cols, :]), in_=in_runs(hidden_sb[:, :, cols])
-            )
+            copy = nc.vector.tensor_copy if n % 2 == 0 else nc.scalar.copy
+            copy(out=regrouped(hidden_grouped[:, cols, :]), in_=in_runs(hidden_sb[:, :, cols]))
 
         def quantise_hidden(n):
             cols = slice(n * N_TILE, (n + 1) * N_TILE)
@@ -152,32 +148,26 @@ def tile_combcrossattention_pa_v_kernel(
 
         def multiply_head(h):
             head_cols = slice(h * D, (h + 1) * D)
-            for first_bank in range(0, N_TILES, BANKS_PER_STORE):
-                out_rows = rows.tile([P, BANKS_PER_STORE, N_TILE], F32)
-                for b in range(BANKS_PER_STORE):
-                    n = first_bank + b
-                    cols = slice(n * N_TILE, (n + 1) * N_TILE)
-                    acc = banks.tile([P, N_TILE], F32)
-                    nc.tensor.matmul_mx(
-                        out=acc[:],
-                        lhsT=dq_codes[:, head_cols].bitcast(E5M2_X4),
-                        lhsT_scale=dq_scales[:, head_cols],
-                        rhs=hidden_codes[:, cols].bitcast(E4M3_X4),
-                        rhs_scale=hidden_scales[:, cols],
-                        start=True,
-                        stop=True,
-                    )
-                    if h == H - 1 and b % 2 == 1:
-                        nc.vector.tensor_copy(out=out_rows[:, b, :], in_=acc[:])
-                    else:
-                        nc.scalar.copy(out=out_rows[:, b, :], in_=acc[:])
-                nc.sync.dma_start(
-                    out=out[head_cols, first_bank * N_TILE : (first_bank + BANKS_PER_STORE) * N_TILE],
-                    in_=out_rows[:].rearrange("p b n -> p (b n)"),
+            out_rows = rows.tile([P, E], F32)
+            for n in range(N_TILES):
+                cols = slice(n * N_TILE, (n + 1) * N_TILE)
+                acc = banks.tile([P, N_TILE], F32)
+                nc.tensor.matmul_mx(
+                    out=acc[:],
+                    lhsT=dq_codes[:, head_cols].bitcast(E5M2_X4),
+                    lhsT_scale=dq_scales[:, head_cols],
+                    rhs=hidden_codes[:, cols].bitcast(E4M3_X4),
+                    rhs_scale=hidden_scales[:, cols],
+                    start=True,
+                    stop=True,
                 )
+                nc.scalar.copy(out=out_rows[:, cols], in_=acc[:])
+            nc.sync.dma_start(out=out[head_cols, :], in_=out_rows[:])
 
         for n in range(N_TILES):
             regroup_hidden(n)
+        for n in range(N_TILES):
+            quantise_hidden(n)
 
         dq = None
         for h in range(H + 1):
@@ -189,10 +179,6 @@ def tile_combcrossattention_pa_v_kernel(
                 coef = coefficient(h, v)
             if h > 0:
                 quantise_head(h - 1, dq_grouped)
-            if 0 <= h - HIDDEN_LAG < N_TILES:
-                quantise_hidden(h - HIDDEN_LAG)
+                multiply_head(h - 1)
             if h < H:
                 dq = head_gradient(h, v, coef)
-
-        for h in range(H):
-            multiply_head(h)

@@ -63,10 +63,11 @@ def tile_combcrossattention_pa_v_kernel(
         nc.vector.memset(gain_row[:], 0.0)
         nc.sync.dma_start(out=gain_row[0:1, :], in_=q_norm_w.unsqueeze(0))
         nc.sync.dma_start(out=rstd_sb[:], in_=rstd.rearrange("(p j) h -> p j h", j=PACK))
+        load_heads(0, 1)
         for part in range(HIDDEN_LOADS):
             cols = slice(part * (E // HIDDEN_LOADS), (part + 1) * (E // HIDDEN_LOADS))
             nc.sync.dma_start(out=hidden_sb[:, :, cols], in_=hidden_view[:, :, cols])
-        first, count = 0, 1
+        first, count = 1, 1
         while first < H:
             load_heads(first, count)
             first, count = first + count, first + count
@@ -164,20 +165,30 @@ def tile_combcrossattention_pa_v_kernel(
                 nc.scalar.copy(out=out_rows[:, cols], in_=acc[:])
             nc.sync.dma_start(out=out[head_cols, :], in_=out_rows[:])
 
-        for n in range(N_TILES):
-            regroup_hidden(n)
-        for n in range(N_TILES):
-            quantise_hidden(n)
+        v = scaled_gradient(0)
+        coef = coefficient(0, v)
+        dq = head_gradient(0, v, coef)
+        regroup_hidden(1)
+        regroup_hidden(3)
+        regroup_hidden(0)
+        dq_grouped = regroup_head(dq)
+        quantise_hidden(0)
+        quantise_head(0, dq_grouped)
+        regroup_hidden(2)
+        quantise_hidden(1)
+        quantise_hidden(2)
+        quantise_hidden(3)
+        multiply_head(0)
 
         dq = None
-        for h in range(H + 1):
+        for h in range(1, H + 1):
             if h < H:
                 v = scaled_gradient(h)
-            if h > 0:
+            if h > 1:
                 dq_grouped = regroup_head(dq)
             if h < H:
                 coef = coefficient(h, v)
-            if h > 0:
+            if h > 1:
                 quantise_head(h - 1, dq_grouped)
                 multiply_head(h - 1)
             if h < H:

@@ -21,6 +21,7 @@ N_TILE = 512
 N_TILES = E // N_TILE
 RUN = 4
 HIDDEN_LOADS = 2
+FIRST_HEADS = 2
 
 FLOPS = 2 * T * H * D * E
 BYTES = 2 * T * E + 2 * D + 4 * T * H * D + 4 * T * H + 2 * H * T * D + 4 * H * D * E
@@ -63,14 +64,15 @@ def tile_combcrossattention_pa_v_kernel(
         nc.vector.memset(gain_row[:], 0.0)
         nc.sync.dma_start(out=gain_row[0:1, :], in_=q_norm_w.unsqueeze(0))
         nc.sync.dma_start(out=rstd_sb[:], in_=rstd.rearrange("(p j) h -> p j h", j=PACK))
-        load_heads(0, 1)
+        for h in range(FIRST_HEADS):
+            load_heads(h, 1)
         for part in range(HIDDEN_LOADS):
             cols = slice(part * (E // HIDDEN_LOADS), (part + 1) * (E // HIDDEN_LOADS))
             nc.sync.dma_start(out=hidden_sb[:, :, cols], in_=hidden_view[:, :, cols])
-        first, count = 1, 1
+        first = FIRST_HEADS
         while first < H:
-            load_heads(first, count)
-            first, count = first + count, first + count
+            load_heads(first, first)
+            first = 2 * first
 
         ones = keep.tile([P, P], BF16)
         nc.vector.memset(ones[:], 1.0)
@@ -104,14 +106,16 @@ def tile_combcrossattention_pa_v_kernel(
         dq_codes = keep.tile([P, H * D], U32, align_bytes=64)
         dq_scales = keep.tile([P, H * D], U8, align_bytes=64)
 
-        def scaled_gradient(h):
+        def new_scaled_gradient():
             v = work.tile([P, PACK, D], F32)
-            for j in range(PACK):
+            return v
+
+        def scaled_gradient(h, v, tokens):
+            for j in tokens:
                 nc.vector.scalar_tensor_tensor(
                     out=v[:, j, :], in0=grad_sb[:, h, j, :], scalar=rstd_sb[:, j, h : h + 1],
                     in1=gain[:], op0=MULT, op1=MULT,
                 )
-            return v
 
         def coefficient(h, v):
             coef = work.tile([P, PACK], F32)
@@ -165,31 +169,46 @@ def tile_combcrossattention_pa_v_kernel(
                 nc.scalar.copy(out=out_rows[:, cols], in_=acc[:])
             nc.sync.dma_start(out=out[head_cols, :], in_=out_rows[:])
 
-        v = scaled_gradient(0)
+        def finish_head(h, v, coef, first_filler, second_filler):
+            dq = head_gradient(h, v, coef)
+            first_filler()
+            dq_grouped = regroup_head(dq)
+            second_filler()
+            quantise_head(h, dq_grouped)
+
+        def finish_head_and_start_next(h, v, coef):
+            v_next = new_scaled_gradient()
+            finish_head(
+                h, v, coef,
+                lambda: scaled_gradient(h + 1, v_next, range(0, PACK // 2)),
+                lambda: scaled_gradient(h + 1, v_next, range(PACK // 2, PACK)),
+            )
+            return v_next
+
+        v = new_scaled_gradient()
+        scaled_gradient(0, v, range(PACK))
         coef = coefficient(0, v)
-        dq = head_gradient(0, v, coef)
+        for h in range(FIRST_HEADS - 1):
+            v = finish_head_and_start_next(h, v, coef)
+            coef = coefficient(h + 1, v)
         regroup_hidden(1)
         regroup_hidden(3)
-        regroup_hidden(0)
-        dq_grouped = regroup_head(dq)
-        quantise_hidden(0)
-        quantise_head(0, dq_grouped)
+        finish_head(
+            FIRST_HEADS - 1, v, coef, lambda: regroup_hidden(0), lambda: quantise_hidden(0)
+        )
         regroup_hidden(2)
         quantise_hidden(1)
         quantise_hidden(2)
         quantise_hidden(3)
-        multiply_head(0)
+        for h in range(FIRST_HEADS):
+            multiply_head(h)
 
-        dq = None
-        for h in range(1, H + 1):
-            if h < H:
-                v = scaled_gradient(h)
-            if h > 1:
-                dq_grouped = regroup_head(dq)
-            if h < H:
-                coef = coefficient(h, v)
-            if h > 1:
-                quantise_head(h - 1, dq_grouped)
-                multiply_head(h - 1)
-            if h < H:
-                dq = head_gradient(h, v, coef)
+        v = new_scaled_gradient()
+        scaled_gradient(FIRST_HEADS, v, range(PACK))
+        coef = coefficient(FIRST_HEADS, v)
+        for h in range(FIRST_HEADS, H - 1):
+            v = finish_head_and_start_next(h, v, coef)
+            multiply_head(h)
+            coef = coefficient(h + 1, v)
+        finish_head(H - 1, v, coef, lambda: None, lambda: None)
+        multiply_head(H - 1)

@@ -22,6 +22,7 @@ N_TILES = E // N_TILE
 RUN = 4
 HIDDEN_LOADS = 2
 FIRST_HEADS = 2
+FIRST_HALF_STORES = H - 3
 
 FLOPS = 2 * T * H * D * E
 BYTES = 2 * T * E + 2 * D + 4 * T * H * D + 4 * T * H + 2 * H * T * D + 4 * H * D * E
@@ -166,8 +167,15 @@ def tile_combcrossattention_pa_v_kernel(
                     start=True,
                     stop=True,
                 )
-                nc.scalar.copy(out=out_rows[:, cols], in_=acc[:])
-            nc.sync.dma_start(out=out[head_cols, :], in_=out_rows[:])
+                if h == H - 1 and n >= N_TILES // 2:
+                    nc.vector.tensor_copy(out=out_rows[:, cols], in_=acc[:])
+                else:
+                    nc.scalar.copy(out=out_rows[:, cols], in_=acc[:])
+                if h >= FIRST_HALF_STORES and n % 2 == 1:
+                    half = slice((n - 1) * N_TILE, (n + 1) * N_TILE)
+                    nc.sync.dma_start(out=out[head_cols, half], in_=out_rows[:, half])
+            if h < FIRST_HALF_STORES:
+                nc.sync.dma_start(out=out[head_cols, :], in_=out_rows[:])
 
         def finish_head(h, v, coef, first_filler, second_filler):
             dq = head_gradient(h, v, coef)

@@ -20,7 +20,6 @@ E = 2048
 N_TILE = 512
 N_TILES = E // N_TILE
 RUN = 4
-HIDDEN_LOADS = 2
 FIRST_HEADS = 2
 FIRST_HALF_STORES = H - 3
 
@@ -56,24 +55,26 @@ def tile_combcrossattention_pa_v_kernel(
         q_view = q.rearrange("(p j) c -> p j c", j=PACK)
         hidden_view = hidden_states.rearrange("(p j) e -> p j e", j=PACK)
 
-        def load_heads(first, count):
-            heads = slice(first, first + count)
-            cols = slice(first * D, (first + count) * D)
+        def load_grad(first, end):
+            heads = slice(first, end)
             nc.sync.dma_start(out=grad_sb[:, heads, :, :], in_=grad_view[:, heads, :, :])
+
+        def load_q(first, end):
+            cols = slice(first * D, end * D)
             nc.sync.dma_start(out=q_sb[:, :, cols], in_=q_view[:, :, cols])
 
         nc.vector.memset(gain_row[:], 0.0)
         nc.sync.dma_start(out=gain_row[0:1, :], in_=q_norm_w.unsqueeze(0))
         nc.sync.dma_start(out=rstd_sb[:], in_=rstd.rearrange("(p j) h -> p j h", j=PACK))
         for h in range(FIRST_HEADS):
-            load_heads(h, 1)
-        for part in range(HIDDEN_LOADS):
-            cols = slice(part * (E // HIDDEN_LOADS), (part + 1) * (E // HIDDEN_LOADS))
-            nc.sync.dma_start(out=hidden_sb[:, :, cols], in_=hidden_view[:, :, cols])
-        first = FIRST_HEADS
-        while first < H:
-            load_heads(first, first)
-            first = 2 * first
+            load_grad(h, h + 1)
+            load_q(h, h + 1)
+        nc.sync.dma_start(out=hidden_sb[:], in_=hidden_view)
+        load_grad(FIRST_HEADS, 2 * FIRST_HEADS)
+        load_q(FIRST_HEADS, 2 * FIRST_HEADS)
+        load_grad(2 * FIRST_HEADS, 4 * FIRST_HEADS)
+        load_q(2 * FIRST_HEADS, H)
+        load_grad(4 * FIRST_HEADS, H)
 
         ones = keep.tile([P, P], BF16)
         nc.vector.memset(ones[:], 1.0)

@@ -44,6 +44,7 @@ def tile_combcrossattention_pa_v_kernel(
         work = ctx.enter_context(tc.tile_pool(name="work", bufs=3))
         rows = ctx.enter_context(tc.tile_pool(name="rows", bufs=4))
         banks = ctx.enter_context(tc.psum_pool(name="banks", bufs=8))
+        ctx.enter_context(tc.manual_schedule(engines={mybir.EngineType.DVE}))
 
         gain_row = keep.tile([P, D], BF16)
         rstd_sb = keep.tile([P, PACK, H], F32)
@@ -119,17 +120,19 @@ def tile_combcrossattention_pa_v_kernel(
                     in1=gain[:], op0=MULT, op1=MULT,
                 )
 
-        def coefficient(h, v):
+        def new_coefficient():
             coef = work.tile([P, PACK], F32)
+            return coef
+
+        def coefficient(h, v, coef, tokens):
             products = work.tile([P, PACK, D], F32)
-            for j in range(PACK):
+            for j in tokens:
                 nc.vector.scalar_tensor_tensor(
                     out=products[:, j, :], in0=v[:, j, :],
                     scalar=minus_r2_over_d[:, j, h : h + 1],
                     in1=q_sb[:, j, h * D : (h + 1) * D], op0=MULT, op1=MULT,
                     accum_out=coef[:, j : j + 1],
                 )
-            return coef
 
         def head_gradient(h, v, coef):
             dq = work.tile([P, PACK, D], BF16)
@@ -178,46 +181,54 @@ def tile_combcrossattention_pa_v_kernel(
             if h < FIRST_HALF_STORES:
                 nc.sync.dma_start(out=out[head_cols, :], in_=out_rows[:])
 
-        def finish_head(h, v, coef, first_filler, second_filler):
-            dq = head_gradient(h, v, coef)
-            first_filler()
-            dq_grouped = regroup_head(dq)
-            second_filler()
-            quantise_head(h, dq_grouped)
+        FIRST_HALF, SECOND_HALF = range(0, PACK // 2), range(PACK // 2, PACK)
+        v, coef = {}, {}
 
-        def finish_head_and_start_next(h, v, coef):
-            v_next = new_scaled_gradient()
-            finish_head(
-                h, v, coef,
-                lambda: scaled_gradient(h + 1, v_next, range(0, PACK // 2)),
-                lambda: scaled_gradient(h + 1, v_next, range(PACK // 2, PACK)),
-            )
-            return v_next
+        def first_pass(h, tokens):
+            if h < H:
+                if h not in v:
+                    v[h] = new_scaled_gradient()
+                scaled_gradient(h, v[h], tokens)
 
-        v = new_scaled_gradient()
-        scaled_gradient(0, v, range(PACK))
-        coef = coefficient(0, v)
-        for h in range(FIRST_HEADS - 1):
-            v = finish_head_and_start_next(h, v, coef)
-            coef = coefficient(h + 1, v)
+        def second_pass(h, tokens):
+            if h < H:
+                if h not in coef:
+                    coef[h] = new_coefficient()
+                coefficient(h, v[h], coef[h], tokens)
+
+        def last_pass(h):
+            return head_gradient(h, v[h], coef[h])
+
+        first_pass(0, range(PACK))
+        second_pass(0, range(PACK))
+        first_pass(1, range(PACK))
+        dq = last_pass(0)
+        second_pass(1, FIRST_HALF)
+        dq_grouped = regroup_head(dq)
+        second_pass(1, SECOND_HALF)
+        quantise_head(0, dq_grouped)
+        dq = last_pass(1)
         regroup_hidden(1)
         regroup_hidden(3)
-        finish_head(
-            FIRST_HEADS - 1, v, coef, lambda: regroup_hidden(0), lambda: quantise_hidden(0)
-        )
+        regroup_hidden(0)
+        dq_grouped = regroup_head(dq)
+        quantise_hidden(0)
+        quantise_head(1, dq_grouped)
         regroup_hidden(2)
         quantise_hidden(1)
+        first_pass(2, range(PACK))
         quantise_hidden(2)
+        second_pass(2, range(PACK))
         quantise_hidden(3)
-        for h in range(FIRST_HEADS):
+        first_pass(3, range(PACK))
+        multiply_head(0)
+        multiply_head(1)
+        for h in range(FIRST_HEADS, H):
+            dq = last_pass(h)
+            first_pass(h + 2, FIRST_HALF)
+            dq_grouped = regroup_head(dq)
+            second_pass(h + 1, FIRST_HALF)
+            quantise_head(h, dq_grouped)
+            second_pass(h + 1, SECOND_HALF)
+            first_pass(h + 2, SECOND_HALF)
             multiply_head(h)
-
-        v = new_scaled_gradient()
-        scaled_gradient(FIRST_HEADS, v, range(PACK))
-        coef = coefficient(FIRST_HEADS, v)
-        for h in range(FIRST_HEADS, H - 1):
-            v = finish_head_and_start_next(h, v, coef)
-            multiply_head(h)
-            coef = coefficient(h + 1, v)
-        finish_head(H - 1, v, coef, lambda: None, lambda: None)
-        multiply_head(H - 1)

@@ -1,6 +1,7 @@
 from contextlib import ExitStack
 
 import concourse.mybir as mybir
+from concourse.masks import make_identity
 
 F32 = mybir.dt.float32
 BF16 = mybir.dt.bfloat16
@@ -19,6 +20,8 @@ D = 128
 E = 2048
 N_TILE = 512
 N_TILES = E // N_TILE
+HIDDEN_LOADS = 2
+BANK_COLS = 256
 RUN = 4
 FIRST_HEADS = 2
 FIRST_HALF_STORES = H - 3
@@ -42,7 +45,7 @@ def tile_combcrossattention_pa_v_kernel(
     with ExitStack() as ctx:
         keep = ctx.enter_context(tc.tile_pool(name="keep", bufs=1))
         work = ctx.enter_context(tc.tile_pool(name="work", bufs=3))
-        rows = ctx.enter_context(tc.tile_pool(name="rows", bufs=4))
+        rows = ctx.enter_context(tc.tile_pool(name="rows", bufs=6))
         banks = ctx.enter_context(tc.psum_pool(name="banks", bufs=8))
         ctx.enter_context(tc.manual_schedule(engines={mybir.EngineType.DVE}))
 
@@ -64,13 +67,17 @@ def tile_combcrossattention_pa_v_kernel(
             cols = slice(first * D, end * D)
             nc.sync.dma_start(out=q_sb[:, :, cols], in_=q_view[:, :, cols])
 
+        identity = keep.tile([P, P], BF16)
+        make_identity(nc, identity[:])
         nc.vector.memset(gain_row[:], 0.0)
         nc.sync.dma_start(out=gain_row[0:1, :], in_=q_norm_w.unsqueeze(0))
         nc.sync.dma_start(out=rstd_sb[:], in_=rstd.rearrange("(p j) h -> p j h", j=PACK))
         for h in range(FIRST_HEADS):
             load_grad(h, h + 1)
             load_q(h, h + 1)
-        nc.sync.dma_start(out=hidden_sb[:], in_=hidden_view)
+        for part in range(HIDDEN_LOADS):
+            cols = slice(part * (E // HIDDEN_LOADS), (part + 1) * (E // HIDDEN_LOADS))
+            nc.sync.dma_start(out=hidden_sb[:, :, cols], in_=hidden_view[:, :, cols])
         load_grad(FIRST_HEADS, 2 * FIRST_HEADS)
         load_q(FIRST_HEADS, 2 * FIRST_HEADS)
         load_grad(2 * FIRST_HEADS, 4 * FIRST_HEADS)
@@ -88,10 +95,29 @@ def tile_combcrossattention_pa_v_kernel(
         hidden_codes = keep.tile([P, E], U32, align_bytes=64)
         hidden_scales = keep.tile([P, E], U8, align_bytes=64)
 
-        def regroup_hidden(n):
+        def regroup_hidden_on_vector(n):
             cols = slice(n * N_TILE, (n + 1) * N_TILE)
-            copy = nc.vector.tensor_copy if n % 2 == 0 else nc.scalar.copy
-            copy(out=regrouped(hidden_grouped[:, cols, :]), in_=in_runs(hidden_sb[:, :, cols]))
+            nc.vector.tensor_copy(
+                out=regrouped(hidden_grouped[:, cols, :]), in_=in_runs(hidden_sb[:, :, cols])
+            )
+
+        def regroup_hidden_on_tensor(n):
+            for first_col in range(n * N_TILE, (n + 1) * N_TILE, BANK_COLS):
+                acc = banks.tile([P, BANK_COLS * PACK], BF16)
+                for k in range(0, BANK_COLS, P):
+                    nc.tensor.matmul(
+                        out=acc[:, k * PACK : (k + P) * PACK].rearrange("p (c j) -> p j c", j=PACK),
+                        lhsT=identity[:],
+                        rhs=hidden_sb[:, :, first_col + k : first_col + k + P],
+                        start=True,
+                        stop=True,
+                    )
+                nc.scalar.copy(
+                    out=hidden_grouped[:, first_col : first_col + BANK_COLS, :].rearrange(
+                        "p c j -> p (c j)"
+                    ),
+                    in_=acc[:],
+                )
 
         def quantise_hidden(n):
             cols = slice(n * N_TILE, (n + 1) * N_TILE)
@@ -156,30 +182,35 @@ def tile_combcrossattention_pa_v_kernel(
                 in_=dq_grouped[:].rearrange("p d j -> p (d j)"),
             )
 
-        def multiply_head(h):
+        def multiply_bank(h, n, out_rows):
             head_cols = slice(h * D, (h + 1) * D)
+            cols = slice(n * N_TILE, (n + 1) * N_TILE)
+            acc = banks.tile([P, N_TILE], F32)
+            nc.tensor.matmul_mx(
+                out=acc[:],
+                lhsT=dq_codes[:, head_cols].bitcast(E5M2_X4),
+                lhsT_scale=dq_scales[:, head_cols],
+                rhs=hidden_codes[:, cols].bitcast(E4M3_X4),
+                rhs_scale=hidden_scales[:, cols],
+                start=True,
+                stop=True,
+            )
+            if h == H - 1 and n >= N_TILES // 2:
+                nc.vector.tensor_copy(out=out_rows[:, cols], in_=acc[:])
+            else:
+                nc.scalar.copy(out=out_rows[:, cols], in_=acc[:])
+
+        def store_columns(h, out_rows, cols):
+            nc.sync.dma_start(out=out[h * D : (h + 1) * D, cols], in_=out_rows[:, cols])
+
+        def multiply_head(h):
             out_rows = rows.tile([P, E], F32)
             for n in range(N_TILES):
-                cols = slice(n * N_TILE, (n + 1) * N_TILE)
-                acc = banks.tile([P, N_TILE], F32)
-                nc.tensor.matmul_mx(
-                    out=acc[:],
-                    lhsT=dq_codes[:, head_cols].bitcast(E5M2_X4),
-                    lhsT_scale=dq_scales[:, head_cols],
-                    rhs=hidden_codes[:, cols].bitcast(E4M3_X4),
-                    rhs_scale=hidden_scales[:, cols],
-                    start=True,
-                    stop=True,
-                )
-                if h == H - 1 and n >= N_TILES // 2:
-                    nc.vector.tensor_copy(out=out_rows[:, cols], in_=acc[:])
-                else:
-                    nc.scalar.copy(out=out_rows[:, cols], in_=acc[:])
+                multiply_bank(h, n, out_rows)
                 if h >= FIRST_HALF_STORES and n % 2 == 1:
-                    half = slice((n - 1) * N_TILE, (n + 1) * N_TILE)
-                    nc.sync.dma_start(out=out[head_cols, half], in_=out_rows[:, half])
+                    store_columns(h, out_rows, slice((n - 1) * N_TILE, (n + 1) * N_TILE))
             if h < FIRST_HALF_STORES:
-                nc.sync.dma_start(out=out[head_cols, :], in_=out_rows[:])
+                store_columns(h, out_rows, slice(0, E))
 
         FIRST_HALF, SECOND_HALF = range(0, PACK // 2), range(PACK // 2, PACK)
         v, coef = {}, {}
@@ -208,21 +239,27 @@ def tile_combcrossattention_pa_v_kernel(
         second_pass(1, SECOND_HALF)
         quantise_head(0, dq_grouped)
         dq = last_pass(1)
-        regroup_hidden(1)
-        regroup_hidden(3)
-        regroup_hidden(0)
+        for n in range(N_TILES - 1):
+            regroup_hidden_on_tensor(n)
         dq_grouped = regroup_head(dq)
-        quantise_hidden(0)
+        regroup_hidden_on_vector(N_TILES - 1)
         quantise_head(1, dq_grouped)
-        regroup_hidden(2)
-        quantise_hidden(1)
+        quantise_hidden(0)
         first_pass(2, range(PACK))
-        quantise_hidden(2)
-        second_pass(2, range(PACK))
         quantise_hidden(3)
+        quantise_hidden(1)
+        second_pass(2, range(PACK))
         first_pass(3, range(PACK))
-        multiply_head(0)
-        multiply_head(1)
+        quantise_hidden(2)
+        first_rows = []
+        for h in range(FIRST_HEADS):
+            out_rows = rows.tile([P, E], F32)
+            first_rows.append(out_rows)
+        for n in (0, 3, 1, 2):
+            for h in range(FIRST_HEADS):
+                multiply_bank(h, n, first_rows[h])
+        for h in range(FIRST_HEADS):
+            store_columns(h, first_rows[h], slice(0, E))
         for h in range(FIRST_HEADS, H):
             dq = last_pass(h)
             first_pass(h + 2, FIRST_HALF)

@@ -26,6 +26,8 @@ RUN = 4
 FIRST_HEADS = 2
 FIRST_HALF_STORES = H - 3
 
+TENSOR_HEADS = range(FIRST_HEADS, H - 2)
+
 FLOPS = 2 * T * H * D * E
 BYTES = 2 * T * E + 2 * D + 4 * T * H * D + 4 * T * H + 2 * H * T * D + 4 * H * D * E
 
@@ -47,7 +49,7 @@ def tile_combcrossattention_pa_v_kernel(
         work = ctx.enter_context(tc.tile_pool(name="work", bufs=3))
         rows = ctx.enter_context(tc.tile_pool(name="rows", bufs=6))
         banks = ctx.enter_context(tc.psum_pool(name="banks", bufs=8))
-        ctx.enter_context(tc.manual_schedule(engines={mybir.EngineType.DVE}))
+        ctx.enter_context(tc.manual_schedule())
 
         gain_row = keep.tile([P, D], BF16)
         rstd_sb = keep.tile([P, PACK, H], F32)
@@ -70,9 +72,11 @@ def tile_combcrossattention_pa_v_kernel(
         identity = keep.tile([P, P], BF16)
         make_identity(nc, identity[:])
         nc.vector.memset(gain_row[:], 0.0)
-        nc.sync.dma_start(out=gain_row[0:1, :], in_=q_norm_w.unsqueeze(0))
         nc.sync.dma_start(out=rstd_sb[:], in_=rstd.rearrange("(p j) h -> p j h", j=PACK))
-        for h in range(FIRST_HEADS):
+        load_grad(0, 1)
+        nc.sync.dma_start(out=gain_row[0:1, :], in_=q_norm_w.unsqueeze(0))
+        load_q(0, 1)
+        for h in range(1, FIRST_HEADS):
             load_grad(h, h + 1)
             load_q(h, h + 1)
         for part in range(HIDDEN_LOADS):
@@ -81,11 +85,14 @@ def tile_combcrossattention_pa_v_kernel(
         load_grad(FIRST_HEADS, 2 * FIRST_HEADS)
         load_q(FIRST_HEADS, 2 * FIRST_HEADS)
         load_grad(2 * FIRST_HEADS, 4 * FIRST_HEADS)
-        load_q(2 * FIRST_HEADS, H)
+        load_q(2 * FIRST_HEADS, 4 * FIRST_HEADS)
         load_grad(4 * FIRST_HEADS, H)
+        load_q(4 * FIRST_HEADS, H)
 
         ones = keep.tile([P, P], BF16)
         nc.vector.memset(ones[:], 1.0)
+        table_loader = keep.tile([P, 1], F32)
+        nc.scalar.copy(out=table_loader[:], in_=ones[:, 0:1])
         acc = banks.tile([P, N_TILE], F32)
         nc.tensor.matmul(out=acc[:, :D], lhsT=ones[:], rhs=gain_row[:], start=True, stop=True)
         gain = keep.tile([P, D], F32)
@@ -169,6 +176,16 @@ def tile_combcrossattention_pa_v_kernel(
                 )
             return dq
 
+        def regroup_head_on_tensor(dq):
+            dq_grouped = work.tile([P, D, PACK], BF16, align_bytes=64)
+            acc = banks.tile([P, D * PACK], BF16)
+            nc.tensor.matmul(
+                out=acc[:].rearrange("p (d j) -> p j d", j=PACK), lhsT=identity[:], rhs=dq[:],
+                start=True, stop=True,
+            )
+            nc.scalar.copy(out=dq_grouped[:].rearrange("p d j -> p (d j)"), in_=acc[:])
+            return dq_grouped
+
         def regroup_head(dq):
             dq_grouped = work.tile([P, D, PACK], BF16, align_bytes=64)
             nc.vector.tensor_copy(out=regrouped(dq_grouped[:]), in_=in_runs(dq[:]))
@@ -239,33 +256,47 @@ def tile_combcrossattention_pa_v_kernel(
         second_pass(1, SECOND_HALF)
         quantise_head(0, dq_grouped)
         dq = last_pass(1)
-        for n in range(N_TILES - 1):
-            regroup_hidden_on_tensor(n)
+        regroup_hidden_on_tensor(0)
+        regroup_hidden_on_tensor(1)
         dq_grouped = regroup_head(dq)
-        regroup_hidden_on_vector(N_TILES - 1)
+        regroup_hidden_on_vector(3)
         quantise_head(1, dq_grouped)
         quantise_hidden(0)
         first_pass(2, range(PACK))
-        quantise_hidden(3)
-        quantise_hidden(1)
-        second_pass(2, range(PACK))
-        first_pass(3, range(PACK))
-        quantise_hidden(2)
         first_rows = []
         for h in range(FIRST_HEADS):
             out_rows = rows.tile([P, E], F32)
             first_rows.append(out_rows)
-        for n in (0, 3, 1, 2):
+
+        def multiply_first_heads(n):
             for h in range(FIRST_HEADS):
                 multiply_bank(h, n, first_rows[h])
+
+        multiply_first_heads(0)
+        regroup_hidden_on_tensor(2)
+        quantise_hidden(3)
+        multiply_first_heads(3)
+        quantise_hidden(1)
+        multiply_first_heads(1)
+        second_pass(2, range(PACK))
+        first_pass(3, range(PACK))
+        quantise_hidden(2)
+        multiply_first_heads(2)
         for h in range(FIRST_HEADS):
             store_columns(h, first_rows[h], slice(0, E))
+        waiting = None
         for h in range(FIRST_HEADS, H):
             dq = last_pass(h)
-            first_pass(h + 2, FIRST_HALF)
-            dq_grouped = regroup_head(dq)
+            regrouping = regroup_head_on_tensor(dq) if h in TENSOR_HEADS else None
+            if waiting is not None:
+                quantise_head(h - 1, waiting)
+                multiply_head(h - 1)
+            waiting = regrouping
             second_pass(h + 1, FIRST_HALF)
-            quantise_head(h, dq_grouped)
+            if h not in TENSOR_HEADS:
+                dq_grouped = regroup_head(dq)
             second_pass(h + 1, SECOND_HALF)
-            first_pass(h + 2, SECOND_HALF)
-            multiply_head(h)
+            if h not in TENSOR_HEADS:
+                quantise_head(h, dq_grouped)
+                multiply_head(h)
+            first_pass(h + 2, range(PACK))

@@ -20,11 +20,10 @@ D = 128
 E = 2048
 N_TILE = 512
 N_TILES = E // N_TILE
-HIDDEN_LOADS = 2
 BANK_COLS = 256
 RUN = 4
 FIRST_HEADS = 2
-FIRST_HALF_STORES = H - 3
+FIRST_HALF_STORES = H - 1
 
 TENSOR_HEADS = range(FIRST_HEADS, H - 2)
 
@@ -79,15 +78,12 @@ def tile_combcrossattention_pa_v_kernel(
         for h in range(1, FIRST_HEADS):
             load_grad(h, h + 1)
             load_q(h, h + 1)
-        for part in range(HIDDEN_LOADS):
-            cols = slice(part * (E // HIDDEN_LOADS), (part + 1) * (E // HIDDEN_LOADS))
-            nc.sync.dma_start(out=hidden_sb[:, :, cols], in_=hidden_view[:, :, cols])
+        nc.sync.dma_start(out=hidden_sb[:], in_=hidden_view)
         load_grad(FIRST_HEADS, 2 * FIRST_HEADS)
         load_q(FIRST_HEADS, 2 * FIRST_HEADS)
         load_grad(2 * FIRST_HEADS, 4 * FIRST_HEADS)
-        load_q(2 * FIRST_HEADS, 4 * FIRST_HEADS)
+        load_q(2 * FIRST_HEADS, H)
         load_grad(4 * FIRST_HEADS, H)
-        load_q(4 * FIRST_HEADS, H)
 
         ones = keep.tile([P, P], BF16)
         nc.vector.memset(ones[:], 1.0)
@@ -259,29 +255,23 @@ def tile_combcrossattention_pa_v_kernel(
         regroup_hidden_on_tensor(0)
         regroup_hidden_on_tensor(1)
         dq_grouped = regroup_head(dq)
-        regroup_hidden_on_vector(3)
+        regroup_hidden_on_vector(2)
         quantise_head(1, dq_grouped)
+        regroup_hidden_on_vector(3)
+        quantise_hidden(2)
         quantise_hidden(0)
         first_pass(2, range(PACK))
+        quantise_hidden(3)
+        quantise_hidden(1)
+        second_pass(2, range(PACK))
+        first_pass(3, range(PACK))
         first_rows = []
         for h in range(FIRST_HEADS):
             out_rows = rows.tile([P, E], F32)
             first_rows.append(out_rows)
-
-        def multiply_first_heads(n):
+        for n in (2, 0, 3, 1):
             for h in range(FIRST_HEADS):
                 multiply_bank(h, n, first_rows[h])
-
-        multiply_first_heads(0)
-        regroup_hidden_on_tensor(2)
-        quantise_hidden(3)
-        multiply_first_heads(3)
-        quantise_hidden(1)
-        multiply_first_heads(1)
-        second_pass(2, range(PACK))
-        first_pass(3, range(PACK))
-        quantise_hidden(2)
-        multiply_first_heads(2)
         for h in range(FIRST_HEADS):
             store_columns(h, first_rows[h], slice(0, E))
         waiting = None

from contextlib import ExitStack

import concourse.mybir as mybir
from concourse.masks import make_identity

F32 = mybir.dt.float32
BF16 = mybir.dt.bfloat16
U32 = mybir.dt.uint32
U8 = mybir.dt.uint8
E4M3_X4 = mybir.dt.float8_e4m3fn_x4
E5M2_X4 = mybir.dt.float8_e5m2_x4
MULT = mybir.AluOpType.mult
ADD = mybir.AluOpType.add

P = 128
PACK = 4
T = P * PACK
H = 16
D = 128
E = 2048
N_TILE = 512
N_TILES = E // N_TILE
BANK_COLS = 256
RUN = 4
FIRST_HEADS = 2
FIRST_HALF_STORES = H - 1

TENSOR_HEADS = range(FIRST_HEADS, H - 2)

FLOPS = 2 * T * H * D * E
BYTES = 2 * T * E + 2 * D + 4 * T * H * D + 4 * T * H + 2 * H * T * D + 4 * H * D * E


def regrouped(by_column):
    return by_column.rearrange("p (c i) j -> p c j i", i=RUN)


def in_runs(by_token):
    return by_token.rearrange("p j (c i) -> p c j i", i=RUN)


def tile_combcrossattention_pa_v_kernel(
    tc, hidden_states, Wq, q_norm_w, q, rstd, grad_out, out
):
    nc = tc.nc
    with ExitStack() as ctx:
        keep = ctx.enter_context(tc.tile_pool(name="keep", bufs=1))
        work = ctx.enter_context(tc.tile_pool(name="work", bufs=3))
        rows = ctx.enter_context(tc.tile_pool(name="rows", bufs=6))
        banks = ctx.enter_context(tc.psum_pool(name="banks", bufs=8))
        ctx.enter_context(tc.manual_schedule())

        gain_row = keep.tile([P, D], BF16)
        rstd_sb = keep.tile([P, PACK, H], F32)
        grad_sb = keep.tile([P, H, PACK, D], BF16)
        q_sb = keep.tile([P, PACK, H * D], F32)
        hidden_sb = keep.tile([P, PACK, E], BF16)

        grad_view = grad_out.rearrange("h (p j) d -> p h j d", j=PACK)
        q_view = q.rearrange("(p j) c -> p j c", j=PACK)
        hidden_view = hidden_states.rearrange("(p j) e -> p j e", j=PACK)

        def load_grad(first, end):
            heads = slice(first, end)
            nc.sync.dma_start(out=grad_sb[:, heads, :, :], in_=grad_view[:, heads, :, :])

        def load_q(first, end):
            cols = slice(first * D, end * D)
            nc.sync.dma_start(out=q_sb[:, :, cols], in_=q_view[:, :, cols])

        identity = keep.tile([P, P], BF16)
        make_identity(nc, identity[:])
        nc.vector.memset(gain_row[:], 0.0)
        nc.sync.dma_start(out=rstd_sb[:], in_=rstd.rearrange("(p j) h -> p j h", j=PACK))
        load_grad(0, 1)
        nc.sync.dma_start(out=gain_row[0:1, :], in_=q_norm_w.unsqueeze(0))
        load_q(0, 1)
        for h in range(1, FIRST_HEADS):
            load_grad(h, h + 1)
            load_q(h, h + 1)
        nc.sync.dma_start(out=hidden_sb[:], in_=hidden_view)
        load_grad(FIRST_HEADS, 2 * FIRST_HEADS)
        load_q(FIRST_HEADS, 2 * FIRST_HEADS)
        load_grad(2 * FIRST_HEADS, 4 * FIRST_HEADS)
        load_q(2 * FIRST_HEADS, H)
        load_grad(4 * FIRST_HEADS, H)

        ones = keep.tile([P, P], BF16)
        nc.vector.memset(ones[:], 1.0)
        table_loader = keep.tile([P, 1], F32)
        nc.scalar.copy(out=table_loader[:], in_=ones[:, 0:1])
        acc = banks.tile([P, N_TILE], F32)
        nc.tensor.matmul(out=acc[:, :D], lhsT=ones[:], rhs=gain_row[:], start=True, stop=True)
        gain = keep.tile([P, D], F32)
        nc.vector.tensor_copy(out=gain[:], in_=acc[:, :D])

        hidden_grouped = keep.tile([P, E, PACK], BF16, align_bytes=64)
        hidden_codes = keep.tile([P, E], U32, align_bytes=64)
        hidden_scales = keep.tile([P, E], U8, align_bytes=64)

        def regroup_hidden_on_vector(n):
            cols = slice(n * N_TILE, (n + 1) * N_TILE)
            nc.vector.tensor_copy(
                out=regrouped(hidden_grouped[:, cols, :]), in_=in_runs(hidden_sb[:, :, cols])
            )

        def regroup_hidden_on_tensor(n):
            for first_col in range(n * N_TILE, (n + 1) * N_TILE, BANK_COLS):
                acc = banks.tile([P, BANK_COLS * PACK], BF16)
                for k in range(0, BANK_COLS, P):
                    nc.tensor.matmul(
                        out=acc[:, k * PACK : (k + P) * PACK].rearrange("p (c j) -> p j c", j=PACK),
                        lhsT=identity[:],
                        rhs=hidden_sb[:, :, first_col + k : first_col + k + P],
                        start=True,
                        stop=True,
                    )
                nc.scalar.copy(
                    out=hidden_grouped[:, first_col : first_col + BANK_COLS, :].rearrange(
                        "p c j -> p (c j)"
                    ),
                    in_=acc[:],
                )

        def quantise_hidden(n):
            cols = slice(n * N_TILE, (n + 1) * N_TILE)
            nc.vector.quantize_mx(
                out=hidden_codes[:, cols].bitcast(E4M3_X4),
                scales=hidden_scales[:, cols],
                in_=hidden_grouped[:, cols, :].rearrange("p w j -> p (w j)"),
            )

        minus_r2_over_d = keep.tile([P, PACK, H], F32)
        nc.vector.scalar_tensor_tensor(
            out=minus_r2_over_d[:], in0=rstd_sb[:], scalar=-1.0 / D, in1=rstd_sb[:],
            op0=MULT, op1=MULT,
        )
        dq_codes = keep.tile([P, H * D], U32, align_bytes=64)
        dq_scales = keep.tile([P, H * D], U8, align_bytes=64)

        def new_scaled_gradient():
            v = work.tile([P, PACK, D], F32)
            return v

        def scaled_gradient(h, v, tokens):
            for j in tokens:
                nc.vector.scalar_tensor_tensor(
                    out=v[:, j, :], in0=grad_sb[:, h, j, :], scalar=rstd_sb[:, j, h : h + 1],
                    in1=gain[:], op0=MULT, op1=MULT,
                )

        def new_coefficient():
            coef = work.tile([P, PACK], F32)
            return coef

        def coefficient(h, v, coef, tokens):
            products = work.tile([P, PACK, D], F32)
            for j in tokens:
                nc.vector.scalar_tensor_tensor(
                    out=products[:, j, :], in0=v[:, j, :],
                    scalar=minus_r2_over_d[:, j, h : h + 1],
                    in1=q_sb[:, j, h * D : (h + 1) * D], op0=MULT, op1=MULT,
                    accum_out=coef[:, j : j + 1],
                )

        def head_gradient(h, v, coef):
            dq = work.tile([P, PACK, D], BF16)
            for j in range(PACK):
                nc.vector.scalar_tensor_tensor(
                    out=dq[:, j, :], in0=q_sb[:, j, h * D : (h + 1) * D],
                    scalar=coef[:, j : j + 1], in1=v[:, j, :], op0=MULT, op1=ADD,
                )
            return dq

        def regroup_head_on_tensor(dq):
            dq_grouped = work.tile([P, D, PACK], BF16, align_bytes=64)
            acc = banks.tile([P, D * PACK], BF16)
            nc.tensor.matmul(
                out=acc[:].rearrange("p (d j) -> p j d", j=PACK), lhsT=identity[:], rhs=dq[:],
                start=True, stop=True,
            )
            nc.scalar.copy(out=dq_grouped[:].rearrange("p d j -> p (d j)"), in_=acc[:])
            return dq_grouped

        def regroup_head(dq):
            dq_grouped = work.tile([P, D, PACK], BF16, align_bytes=64)
            nc.vector.tensor_copy(out=regrouped(dq_grouped[:]), in_=in_runs(dq[:]))
            return dq_grouped

        def quantise_head(h, dq_grouped):
            cols = slice(h * D, (h + 1) * D)
            nc.vector.quantize_mx(
                out=dq_codes[:, cols].bitcast(E5M2_X4),
                scales=dq_scales[:, cols],
                in_=dq_grouped[:].rearrange("p d j -> p (d j)"),
            )

        def multiply_bank(h, n, out_rows):
            head_cols = slice(h * D, (h + 1) * D)
            cols = slice(n * N_TILE, (n + 1) * N_TILE)
            acc = banks.tile([P, N_TILE], F32)
            nc.tensor.matmul_mx(
                out=acc[:],
                lhsT=dq_codes[:, head_cols].bitcast(E5M2_X4),
                lhsT_scale=dq_scales[:, head_cols],
                rhs=hidden_codes[:, cols].bitcast(E4M3_X4),
                rhs_scale=hidden_scales[:, cols],
                start=True,
                stop=True,
            )
            if h == H - 1 and n >= N_TILES // 2:
                nc.vector.tensor_copy(out=out_rows[:, cols], in_=acc[:])
            else:
                nc.scalar.copy(out=out_rows[:, cols], in_=acc[:])

        def store_columns(h, out_rows, cols):
            nc.sync.dma_start(out=out[h * D : (h + 1) * D, cols], in_=out_rows[:, cols])

        def multiply_head(h):
            out_rows = rows.tile([P, E], F32)
            for n in range(N_TILES):
                multiply_bank(h, n, out_rows)
                if h >= FIRST_HALF_STORES and n % 2 == 1:
                    store_columns(h, out_rows, slice((n - 1) * N_TILE, (n + 1) * N_TILE))
            if h < FIRST_HALF_STORES:
                store_columns(h, out_rows, slice(0, E))

        FIRST_HALF, SECOND_HALF = range(0, PACK // 2), range(PACK // 2, PACK)
        v, coef = {}, {}

        def first_pass(h, tokens):
            if h < H:
                if h not in v:
                    v[h] = new_scaled_gradient()
                scaled_gradient(h, v[h], tokens)

        def second_pass(h, tokens):
            if h < H:
                if h not in coef:
                    coef[h] = new_coefficient()
                coefficient(h, v[h], coef[h], tokens)

        def last_pass(h):
            return head_gradient(h, v[h], coef[h])

        first_pass(0, range(PACK))
        second_pass(0, range(PACK))
        first_pass(1, range(PACK))
        dq = last_pass(0)
        second_pass(1, FIRST_HALF)
        dq_grouped = regroup_head(dq)
        second_pass(1, SECOND_HALF)
        quantise_head(0, dq_grouped)
        dq = last_pass(1)
        regroup_hidden_on_tensor(0)
        regroup_hidden_on_tensor(1)
        dq_grouped = regroup_head(dq)
        regroup_hidden_on_vector(2)
        quantise_head(1, dq_grouped)
        regroup_hidden_on_vector(3)
        quantise_hidden(2)
        quantise_hidden(0)
        first_pass(2, range(PACK))
        quantise_hidden(3)
        quantise_hidden(1)
        second_pass(2, range(PACK))
        first_pass(3, range(PACK))
        first_rows = []
        for h in range(FIRST_HEADS):
            out_rows = rows.tile([P, E], F32)
            first_rows.append(out_rows)
        for n in (2, 0, 3, 1):
            for h in range(FIRST_HEADS):
                multiply_bank(h, n, first_rows[h])
        for h in range(FIRST_HEADS):
            store_columns(h, first_rows[h], slice(0, E))
        waiting = None
        for h in range(FIRST_HEADS, H):
            dq = last_pass(h)
            regrouping = regroup_head_on_tensor(dq) if h in TENSOR_HEADS else None
            if waiting is not None:
                quantise_head(h - 1, waiting)
                multiply_head(h - 1)
            waiting = regrouping
            second_pass(h + 1, FIRST_HALF)
            if h not in TENSOR_HEADS:
                dq_grouped = regroup_head(dq)
            second_pass(h + 1, SECOND_HALF)
            if h not in TENSOR_HEADS:
                quantise_head(h, dq_grouped)
                multiply_head(h)
            first_pass(h + 2, range(PACK))
